import numpy as np
import ml_dtypes


def mxq(x, axis, fmt="e4m3"):
    dtype, down = {"e4m3": (ml_dtypes.float8_e4m3fn, 7), "e5m2": (ml_dtypes.float8_e5m2, 14)}[fmt]
    v = np.moveaxis(np.asarray(x, np.float32).astype(ml_dtypes.bfloat16).astype(np.float64), axis, -1)
    blocks = v.reshape(v.shape[:-1] + (-1, 32))
    amax = np.abs(blocks).max(-1, keepdims=True)
    byte = np.maximum(np.where(amax > 0, np.frexp(amax)[1] - 1 + 127, 0) - down, 1)
    scale = np.exp2(byte - 127.0)
    codes = (blocks / scale).astype(np.float32).astype(dtype).astype(np.float64)
    return np.moveaxis((codes * scale).reshape(v.shape), -1, axis)


WIDE = False


def mx_kscale(k):
    if not WIDE:
        return np.ones(k)
    levels = np.array([10, -10, 5, -5, 0])
    if k % 512:
        return np.exp2(np.random.permutation(np.resize(levels, k // 32))).repeat(32)
    a = np.empty((k // 512, 16))
    for p in range(k // 512):
        a[p, :8] = np.random.permutation(np.resize(levels, 8))
        for g in range(8):
            far = levels[np.abs(levels - a[p, g]) >= 10]
            a[p, g + 8] = far[np.random.randint(len(far))]
    return np.exp2(a.ravel()).repeat(32)


BF16 = ml_dtypes.bfloat16


def bf(x):
    return np.asarray(x, np.float32).astype(BF16)


def f64(x):
    return np.asarray(x).astype(np.float64)


B, S, D, H = 1, 1024, 512, 512


def setup_inputs():
    s, t = mx_kscale(D), mx_kscale(H)
    return {"audio_feature": bf(np.random.standard_normal((B, S, D)) * s),
            "W_phi": bf(np.random.standard_normal((D, H)) / np.sqrt(D) / s[:, None] * t),
            "b_phi": bf(np.random.standard_normal(H) * 0.2 * t),
            "W_theta": bf(np.random.standard_normal((D, H)) / np.sqrt(D) / s[:, None] / t),
            "b_theta": bf(np.random.standard_normal(H) * 0.2 / t)}


def reference(audio_feature, W_phi, b_phi, W_theta, b_theta):
    xq = mxq(f64(audio_feature), 2, "e4m3")
    phi_a = (xq @ mxq(f64(W_phi), 0, "e4m3")) + f64(b_phi)
    theta_a = (xq @ mxq(f64(W_theta), 0, "e4m3")) + f64(b_theta)
    scores = (mxq(phi_a, 2, "e4m3") @ mxq(theta_a, 2, "e4m3").transpose(0, 2, 1)) / np.sqrt(D)
    scores = np.maximum(scores, 0.0)
    return (scores + scores.transpose(0, 2, 1)) * 0.5

@@ -1,0 +1,240 @@
+import math
+
+import concourse.mybir as mybir
+from concourse.masks import make_identity
+
+F32 = mybir.dt.float32
+BF16 = mybir.dt.bfloat16
+U32 = mybir.dt.uint32
+U8 = mybir.dt.uint8
+FP8X4 = mybir.dt.float8_e4m3fn_x4
+ACT = mybir.ActivationFunctionType
+ALU = mybir.AluOpType
+
+P = 128
+PACK = 4
+S = 1024
+D = 512
+H = 512
+BANK = 512
+HALVES = S // BANK
+TILES = BANK // P
+PAIR = 2 * P
+PAIRS = S // PAIR
+PHI = 0
+THETA = 1
+RESULT_SCALE = 0.5 / math.sqrt(D)
+
+FLOPS = 2 * (2 * S * D * H) + 2 * S * S * H
+
+
+def regroup_and_quantise(nc, planes, grouped, codes, scales, pieces):
+    columns = codes.shape[1]
+    width = columns // pieces
+    source = planes[:].rearrange("p (t c i) -> p c t i", i=4, t=PACK)
+    target = grouped[:].rearrange("p (c i t) -> p c t i", i=4, t=PACK)
+    for piece in range(pieces + 1):
+        if piece < pieces:
+            runs = slice(piece * width // 4, (piece + 1) * width // 4)
+            nc.vector.tensor_copy(out=target[:, runs], in_=source[:, runs])
+        if piece > 0:
+            cols = slice((piece - 1) * width, piece * width)
+            nc.vector.quantize_mx(
+                out=codes[:, cols].bitcast(FP8X4),
+                scales=scales[:, cols],
+                in_=grouped[:, (piece - 1) * width * PACK : piece * width * PACK],
+            )
+
+
+def tile_selfattention_pa_kernel(tc, audio_feature, W_phi, b_phi, W_theta, b_theta, out):
+    nc = tc.nc
+    x = audio_feature.flatten_outer_dims()
+    result = out.flatten_outer_dims()
+    weights = (W_phi, W_theta)
+    biases = (b_phi, b_theta)
+
+    with tc.tile_pool(name="keep", bufs=1) as keep, tc.psum_pool(name="psum", bufs=8) as psum:
+        identity = keep.tile([P, P], F32)
+        bias_cols = [keep.tile([P, PACK], BF16, name="bias_cols%d" % o) for o in (PHI, THETA)]
+
+        x_raw = [keep.tile([P, 2 * D], BF16, name="x_raw%d" % g) for g in range(PAIRS)]
+        x_grouped = [
+            keep.tile([P, PAIR * PACK], BF16, name="x_grouped%d" % g, align_bytes=64) for g in range(PAIRS)
+        ]
+        x_codes = [keep.tile([P, BANK], U32, name="x_codes%d" % h, align_bytes=64) for h in range(HALVES)]
+        x_scales = [keep.tile([P, BANK], U8, name="x_scales%d" % h, align_bytes=64) for h in range(HALVES)]
+
+        w_raw = [keep.tile([P, PACK * H], BF16, name="w_raw%d" % o) for o in (PHI, THETA)]
+        w_grouped = [keep.tile([P, H * PACK], BF16, name="w_grouped%d" % o, align_bytes=64) for o in (PHI, THETA)]
+        w_codes = [keep.tile([P, H], U32, name="w_codes%d" % o, align_bytes=64) for o in (PHI, THETA)]
+        w_scales = [keep.tile([P, H], U8, name="w_scales%d" % o, align_bytes=64) for o in (PHI, THETA)]
+
+        proj_planes = [
+            [keep.tile([P, PACK * BANK], BF16, name="proj_planes%d_%d" % (o, h)) for h in range(HALVES)]
+            for o in (PHI, THETA)
+        ]
+        proj_grouped = [
+            [keep.tile([P, BANK * PACK], BF16, name="proj_grouped%d_%d" % (o, h), align_bytes=64) for h in range(HALVES)]
+            for o in (PHI, THETA)
+        ]
+        proj_codes = [
+            [keep.tile([P, BANK], U32, name="proj_codes%d_%d" % (o, h), align_bytes=64) for h in range(HALVES)]
+            for o in (PHI, THETA)
+        ]
+        proj_scales = [
+            [keep.tile([P, BANK], U8, name="proj_scales%d_%d" % (o, h), align_bytes=64) for h in range(HALVES)]
+            for o in (PHI, THETA)
+        ]
+
+        r_half = [
+            [keep.tile([P, BANK], F32, name="r_half%d_%d" % (i, h)) for h in range(HALVES)] for i in range(S // P)
+        ]
+        out_half = [
+            [keep.tile([P, BANK], F32, name="out_half%d_%d" % (i, h)) for h in range(HALVES)] for i in range(S // P)
+        ]
+
+        def load_x(g):
+            nc.sync.dma_start(
+                out=x_raw[g][:].rearrange("p (t d) -> p t d", t=2),
+                in_=x[g * PAIR : (g + 1) * PAIR, :].rearrange("(t p) d -> p t d", p=P),
+            )
+
+        def load_weight(o):
+            nc.sync.dma_start(
+                out=w_raw[o][:].rearrange("p (j h) -> p j h", j=PACK),
+                in_=weights[o].rearrange("(p j) h -> p j h", j=PACK),
+            )
+
+        def load_bias():
+            for o in (PHI, THETA):
+                nc.sync.dma_start(out=bias_cols[o][:], in_=biases[o].rearrange("(p j) -> p j", j=PACK))
+
+        def quantise_weight(o):
+            source = w_raw[o][:].rearrange("p (j m t) -> p t m j", j=PACK, t=PACK)
+            target = w_grouped[o][:].rearrange("p (t m j) -> p t m j", t=PACK, j=PACK)
+            for t in range(PACK + 1):
+                if t < PACK:
+                    nc.vector.tensor_copy(out=target[:, t], in_=source[:, t])
+                if t > 0:
+                    cols = slice((t - 1) * P, t * P)
+                    nc.vector.quantize_mx(
+                        out=w_codes[o][:, cols].bitcast(FP8X4),
+                        scales=w_scales[o][:, cols],
+                        in_=w_grouped[o][:, (t - 1) * P * PACK : t * P * PACK],
+                    )
+
+        def transpose_x(g):
+            words = x_raw[g][:].bitcast(F32)
+            bank = psum.tile([P, BANK], F32, name="bank", tag="bank")
+            for t in range(2):
+                for u in range(2):
+                    tu = 2 * t + u
+                    nc.tensor.transpose(
+                        bank[:, tu * P : (tu + 1) * P], words[:, 2 * P * t + u : 2 * P * (t + 1) : 2], identity[:]
+                    )
+            nc.scalar.copy(
+                out=x_grouped[g][:].bitcast(F32).rearrange("p (t s u) -> p t s u", t=2, u=2),
+                in_=bank[:].rearrange("p (t u s) -> p t s u", t=2, u=2),
+            )
+
+        def quantise_x(g):
+            half, cols = g // 2, slice((g % 2) * PAIR, (g % 2 + 1) * PAIR)
+            nc.vector.quantize_mx(
+                out=x_codes[half][:, cols].bitcast(FP8X4), scales=x_scales[half][:, cols], in_=x_grouped[g][:]
+            )
+
+        def project(o, half):
+            for j in range(PACK):
+                cols = slice(j * P, (j + 1) * P)
+                bank = psum.tile([P, BANK], F32, name="bank", tag="bank")
+                nc.tensor.matmul_mx(
+                    out=bank[:],
+                    lhsT=w_codes[o][:, cols].bitcast(FP8X4),
+                    lhsT_scale=w_scales[o][:, cols],
+                    rhs=x_codes[half][:].bitcast(FP8X4),
+                    rhs_scale=x_scales[half][:],
+                    start=True,
+                    stop=True,
+                )
+                plane = proj_planes[o][half][:, j * BANK : (j + 1) * BANK]
+                bias = bias_cols[o][:, j : j + 1]
+                if o == THETA and j == PACK - 1:
+                    nc.vector.tensor_scalar(out=plane, in0=bank[:], scalar1=bias, scalar2=None, op0=ALU.add)
+                else:
+                    nc.scalar.activation(out=plane, in_=bank[:], func=ACT.Identity, bias=bias, scale=1.0)
+
+        def quantise_projection(o, half):
+            regroup_and_quantise(
+                nc, proj_planes[o][half], proj_grouped[o][half], proj_codes[o][half], proj_scales[o][half], pieces=2
+            )
+
+        def scores(row_half, col_half):
+            for k in range(TILES):
+                cols = slice(k * P, (k + 1) * P)
+                bank = psum.tile([P, BANK], F32, name="bank", tag="bank")
+                nc.tensor.matmul_mx(
+                    out=bank[:],
+                    lhsT=proj_codes[PHI][row_half][:, cols].bitcast(FP8X4),
+                    lhsT_scale=proj_scales[PHI][row_half][:, cols],
+                    rhs=proj_codes[THETA][col_half][:].bitcast(FP8X4),
+                    rhs_scale=proj_scales[THETA][col_half][:],
+                    start=True,
+                    stop=True,
+                )
+                nc.scalar.activation(
+                    out=r_half[row_half * TILES + k][col_half][:], in_=bank[:], func=ACT.Relu, scale=RESULT_SCALE
+                )
+
+        def symmetrise(row_half, col_half):
+            for k in range(TILES):
+                i = row_half * TILES + k
+                bank = psum.tile([P, BANK], F32, name="bank", tag="bank")
+                for m in range(TILES):
+                    nc.tensor.transpose(
+                        bank[:, m * P : (m + 1) * P],
+                        r_half[col_half * TILES + m][row_half][:, k * P : (k + 1) * P],
+                        identity[:],
+                    )
+                nc.vector.tensor_tensor(out=out_half[i][col_half][:], in0=bank[:], in1=r_half[i][col_half][:], op=ALU.add)
+                nc.sync.dma_start(
+                    out=result[i * P : (i + 1) * P, col_half * BANK : (col_half + 1) * BANK], in_=out_half[i][col_half][:]
+                )
+
+        with tc.manual_schedule():
+            make_identity(nc, identity[:])
+            load_x(0)
+            load_x(1)
+            load_bias()
+            load_weight(PHI)
+            load_x(2)
+            load_x(3)
+            load_weight(THETA)
+
+            transpose_x(0)
+            transpose_x(1)
+            quantise_x(0)
+            quantise_x(1)
+            quantise_weight(PHI)
+            transpose_x(2)
+            transpose_x(3)
+            quantise_x(2)
+            quantise_x(3)
+
+            project(PHI, 0)
+            quantise_weight(THETA)
+            quantise_projection(PHI, 0)
+            project(THETA, 0)
+            project(PHI, 1)
+            quantise_projection(THETA, 0)
+            quantise_projection(PHI, 1)
+            project(THETA, 1)
+
+            scores(0, 0)
+            scores(1, 0)
+            quantise_projection(THETA, 1)
+            symmetrise(0, 0)
+            scores(0, 1)
+            symmetrise(0, 1)
+            scores(1, 1)
+            symmetrise(1, 0)
+            symmetrise(1, 1)

@@ -17,33 +17,13 @@ S = 1024
 D = 512
 H = 512
 BANK = 512
-HALVES = S // BANK
-TILES = BANK // P
-PAIR = 2 * P
-PAIRS = S // PAIR
+Q = 2 * P
+QUARTERS = S // Q
 PHI = 0
 THETA = 1
 RESULT_SCALE = 0.5 / math.sqrt(D)
 
 FLOPS = 2 * (2 * S * D * H) + 2 * S * S * H
-
-
-def regroup_and_quantise(nc, planes, grouped, codes, scales, pieces):
-    columns = codes.shape[1]
-    width = columns // pieces
-    source = planes[:].rearrange("p (t c i) -> p c t i", i=4, t=PACK)
-    target = grouped[:].rearrange("p (c i t) -> p c t i", i=4, t=PACK)
-    for piece in range(pieces + 1):
-        if piece < pieces:
-            runs = slice(piece * width // 4, (piece + 1) * width // 4)
-            nc.vector.tensor_copy(out=target[:, runs], in_=source[:, runs])
-        if piece > 0:
-            cols = slice((piece - 1) * width, piece * width)
-            nc.vector.quantize_mx(
-                out=codes[:, cols].bitcast(FP8X4),
-                scales=scales[:, cols],
-                in_=grouped[:, (piece - 1) * width * PACK : piece * width * PACK],
-            )
 
 
 def tile_selfattention_pa_kernel(tc, audio_feature, W_phi, b_phi, W_theta, b_theta, out):
@@ -54,49 +34,31 @@ def tile_selfattention_pa_kernel(tc, audio_feature, W_phi, b_phi, W_theta, b_the
     biases = (b_phi, b_theta)
 
     with tc.tile_pool(name="keep", bufs=1) as keep, tc.psum_pool(name="psum", bufs=8) as psum:
+        def per_quarter(name, width, dtype):
+            return [keep.tile([P, width], dtype, name="%s%d" % (name, q), align_bytes=64) for q in range(QUARTERS)]
+
         identity = keep.tile([P, P], F32)
         bias_cols = [keep.tile([P, PACK], BF16, name="bias_cols%d" % o) for o in (PHI, THETA)]
 
-        x_raw = [keep.tile([P, 2 * D], BF16, name="x_raw%d" % g) for g in range(PAIRS)]
-        x_grouped = [
-            keep.tile([P, PAIR * PACK], BF16, name="x_grouped%d" % g, align_bytes=64) for g in range(PAIRS)
-        ]
-        x_codes = [keep.tile([P, BANK], U32, name="x_codes%d" % h, align_bytes=64) for h in range(HALVES)]
-        x_scales = [keep.tile([P, BANK], U8, name="x_scales%d" % h, align_bytes=64) for h in range(HALVES)]
+        x_raw = per_quarter("x_raw", 2 * D, BF16)
+        x_grouped = per_quarter("x_grouped", Q * PACK, BF16)
+        x_codes = per_quarter("x_codes", Q, U32)
+        x_scales = per_quarter("x_scales", Q, U8)
 
         w_raw = [keep.tile([P, PACK * H], BF16, name="w_raw%d" % o) for o in (PHI, THETA)]
         w_grouped = [keep.tile([P, H * PACK], BF16, name="w_grouped%d" % o, align_bytes=64) for o in (PHI, THETA)]
         w_codes = [keep.tile([P, H], U32, name="w_codes%d" % o, align_bytes=64) for o in (PHI, THETA)]
         w_scales = [keep.tile([P, H], U8, name="w_scales%d" % o, align_bytes=64) for o in (PHI, THETA)]
 
-        proj_planes = [
-            [keep.tile([P, PACK * BANK], BF16, name="proj_planes%d_%d" % (o, h)) for h in range(HALVES)]
-            for o in (PHI, THETA)
-        ]
-        proj_grouped = [
-            [keep.tile([P, BANK * PACK], BF16, name="proj_grouped%d_%d" % (o, h), align_bytes=64) for h in range(HALVES)]
-            for o in (PHI, THETA)
-        ]
-        proj_codes = [
-            [keep.tile([P, BANK], U32, name="proj_codes%d_%d" % (o, h), align_bytes=64) for h in range(HALVES)]
-            for o in (PHI, THETA)
-        ]
-        proj_scales = [
-            [keep.tile([P, BANK], U8, name="proj_scales%d_%d" % (o, h), align_bytes=64) for h in range(HALVES)]
-            for o in (PHI, THETA)
-        ]
+        proj_planes = [per_quarter("proj_planes%d_" % o, PACK * Q, BF16) for o in (PHI, THETA)]
+        proj_grouped = [per_quarter("proj_grouped%d_" % o, Q * PACK, BF16) for o in (PHI, THETA)]
+        proj_codes = [per_quarter("proj_codes%d_" % o, Q, U32) for o in (PHI, THETA)]
+        proj_scales = [per_quarter("proj_scales%d_" % o, Q, U8) for o in (PHI, THETA)]
 
-        r_half = [
-            [keep.tile([P, BANK], F32, name="r_half%d_%d" % (i, h)) for h in range(HALVES)] for i in range(S // P)
-        ]
-        out_half = [
-            [keep.tile([P, BANK], F32, name="out_half%d_%d" % (i, h)) for h in range(HALVES)] for i in range(S // P)
-        ]
-
-        def load_x(g):
+        def load_x(q):
             nc.sync.dma_start(
-                out=x_raw[g][:].rearrange("p (t d) -> p t d", t=2),
-                in_=x[g * PAIR : (g + 1) * PAIR, :].rearrange("(t p) d -> p t d", p=P),
+                out=x_raw[q][:].rearrange("p (t d) -> p t d", t=2),
+                in_=x[q * Q : (q + 1) * Q, :].rearrange("(t p) d -> p t d", p=P),
             )
 
         def load_weight(o):
@@ -109,132 +71,315 @@ def tile_selfattention_pa_kernel(tc, audio_feature, W_phi, b_phi, W_theta, b_the
             for o in (PHI, THETA):
                 nc.sync.dma_start(out=bias_cols[o][:], in_=biases[o].rearrange("(p j) -> p j", j=PACK))
 
-        def quantise_weight(o):
-            source = w_raw[o][:].rearrange("p (j m t) -> p t m j", j=PACK, t=PACK)
-            target = w_grouped[o][:].rearrange("p (t m j) -> p t m j", t=PACK, j=PACK)
-            for t in range(PACK + 1):
-                if t < PACK:
-                    nc.vector.tensor_copy(out=target[:, t], in_=source[:, t])
-                if t > 0:
-                    cols = slice((t - 1) * P, t * P)
-                    nc.vector.quantize_mx(
-                        out=w_codes[o][:, cols].bitcast(FP8X4),
-                        scales=w_scales[o][:, cols],
-                        in_=w_grouped[o][:, (t - 1) * P * PACK : t * P * PACK],
-                    )
+        def copy(engine, target, source):
+            if engine is nc.scalar:
+                nc.scalar.copy(out=target, in_=source)
+            else:
+                nc.vector.tensor_copy(out=target, in_=source)
 
-        def transpose_x(g):
-            words = x_raw[g][:].bitcast(F32)
-            bank = psum.tile([P, BANK], F32, name="bank", tag="bank")
+        def new_bank():
+            return psum.tile([P, BANK], F32, name="bank", tag="bank")
+
+        def regroup_weight(o, t, engine):
+            copy(
+                engine,
+                w_grouped[o][:].rearrange("p (t m j) -> p t m j", t=PACK, j=PACK)[:, t],
+                w_raw[o][:].rearrange("p (j m t) -> p t m j", j=PACK, t=PACK)[:, t],
+            )
+
+        def quantise_weight(o, t):
+            cols = slice(t * P, (t + 1) * P)
+            nc.vector.quantize_mx(
+                out=w_codes[o][:, cols].bitcast(FP8X4),
+                scales=w_scales[o][:, cols],
+                in_=w_grouped[o][:, t * P * PACK : (t + 1) * P * PACK],
+            )
+
+        banks = {}
+
+        def transpose_x(q):
+            words = x_raw[q][:].bitcast(F32)
+            bank = banks["x", q] = new_bank()
             for t in range(2):
                 for u in range(2):
                     tu = 2 * t + u
                     nc.tensor.transpose(
                         bank[:, tu * P : (tu + 1) * P], words[:, 2 * P * t + u : 2 * P * (t + 1) : 2], identity[:]
                     )
-            nc.scalar.copy(
-                out=x_grouped[g][:].bitcast(F32).rearrange("p (t s u) -> p t s u", t=2, u=2),
-                in_=bank[:].rearrange("p (t u s) -> p t s u", t=2, u=2),
+
+        def regroup_x(q, engine):
+            copy(
+                engine,
+                x_grouped[q][:].bitcast(F32).rearrange("p (t s u) -> p t s u", t=2, u=2),
+                banks["x", q][:].rearrange("p (t u s) -> p t s u", t=2, u=2),
             )
 
-        def quantise_x(g):
-            half, cols = g // 2, slice((g % 2) * PAIR, (g % 2 + 1) * PAIR)
+        def quantise_x(q):
+            nc.vector.quantize_mx(out=x_codes[q][:].bitcast(FP8X4), scales=x_scales[q][:], in_=x_grouped[q][:])
+
+        def project_part(o, q, t, positions, part):
+            nc.tensor.matmul_mx(
+                out=part,
+                lhsT=w_codes[o][:, t * P : (t + 1) * P].bitcast(FP8X4),
+                lhsT_scale=w_scales[o][:, t * P : (t + 1) * P],
+                rhs=x_codes[q][:, positions].bitcast(FP8X4),
+                rhs_scale=x_scales[q][:, positions],
+                start=True,
+                stop=True,
+            )
+
+        def project(o, q):
+            for t in range(PACK):
+                if t % 2 == 0:
+                    bank = new_bank()
+                banks["plane", o, q, t] = bank[:, t % 2 * Q : (t % 2 + 1) * Q]
+                project_part(o, q, t, slice(0, Q), banks["plane", o, q, t])
+
+        def add_bias(o, q, t):
+            nc.scalar.activation(
+                out=proj_planes[o][q][:, t * Q : (t + 1) * Q],
+                in_=banks["plane", o, q, t],
+                func=ACT.Identity,
+                bias=bias_cols[o][:, t : t + 1],
+                scale=1.0,
+            )
+
+        def regroup(o, q):
+            nc.vector.tensor_copy(
+                out=proj_grouped[o][q][:].rearrange("p (c i t) -> p c t i", i=4, t=PACK),
+                in_=proj_planes[o][q][:].rearrange("p (t c i) -> p c t i", i=4, t=PACK),
+            )
+
+        def project_words(o, q):
+            for k in range(2):
+                bank = banks["words", o, q, k] = new_bank()
+                for t in range(PACK):
+                    project_part(o, q, t, slice(k * P, (k + 1) * P), bank[:, t * P : (t + 1) * P])
+
+        def add_bias_words(o, q, k):
+            nc.vector.tensor_tensor(
+                out=proj_grouped[o][q][:, k * BANK : (k + 1) * BANK].rearrange("p (c t) -> p c t", t=PACK),
+                in0=banks["words", o, q, k][:].rearrange("p (t c) -> p c t", t=PACK),
+                in1=bias_cols[o][:].unsqueeze(1).to_broadcast([P, P, PACK]),
+                op=ALU.add,
+            )
+
+        def quantise(o, q):
             nc.vector.quantize_mx(
-                out=x_codes[half][:, cols].bitcast(FP8X4), scales=x_scales[half][:, cols], in_=x_grouped[g][:]
+                out=proj_codes[o][q][:].bitcast(FP8X4), scales=proj_scales[o][q][:], in_=proj_grouped[o][q][:]
             )
 
-        def project(o, half):
-            for j in range(PACK):
-                cols = slice(j * P, (j + 1) * P)
-                bank = psum.tile([P, BANK], F32, name="bank", tag="bank")
+        def product(lhs, rhs, q, n):
+            bank = banks["product", lhs, q, n] = new_bank()
+            for k in range(2):
+                rows = slice(k * P, (k + 1) * P)
                 nc.tensor.matmul_mx(
-                    out=bank[:],
-                    lhsT=w_codes[o][:, cols].bitcast(FP8X4),
-                    lhsT_scale=w_scales[o][:, cols],
-                    rhs=x_codes[half][:].bitcast(FP8X4),
-                    rhs_scale=x_scales[half][:],
+                    out=bank[:, k * Q : (k + 1) * Q],
+                    lhsT=proj_codes[lhs][q][:, rows].bitcast(FP8X4),
+                    lhsT_scale=proj_scales[lhs][q][:, rows],
+                    rhs=proj_codes[rhs][n][:].bitcast(FP8X4),
+                    rhs_scale=proj_scales[rhs][n][:],
                     start=True,
                     stop=True,
                 )
-                plane = proj_planes[o][half][:, j * BANK : (j + 1) * BANK]
-                bias = bias_cols[o][:, j : j + 1]
-                if o == THETA and j == PACK - 1:
-                    nc.vector.tensor_scalar(out=plane, in0=bank[:], scalar1=bias, scalar2=None, op0=ALU.add)
-                else:
-                    nc.scalar.activation(out=plane, in_=bank[:], func=ACT.Identity, bias=bias, scale=1.0)
 
-        def quantise_projection(o, half):
-            regroup_and_quantise(
-                nc, proj_planes[o][half], proj_grouped[o][half], proj_codes[o][half], proj_scales[o][half], pieces=2
+        tiles = {}
+
+        def new_tile(name, q, n):
+            tiles[name, q, n] = keep.tile([P, BANK], F32, name="%s_%d_%d" % (name, q, n))
+            return tiles[name, q, n]
+
+        def store(q, n, tile):
+            nc.sync.dma_start(
+                out=result[q * Q : (q + 1) * Q, n * Q : (n + 1) * Q].rearrange("(k p) c -> p k c", p=P),
+                in_=tile[:].rearrange("p (k c) -> p k c", k=2),
             )
 
-        def scores(row_half, col_half):
-            for k in range(TILES):
-                cols = slice(k * P, (k + 1) * P)
-                bank = psum.tile([P, BANK], F32, name="bank", tag="bank")
-                nc.tensor.matmul_mx(
-                    out=bank[:],
-                    lhsT=proj_codes[PHI][row_half][:, cols].bitcast(FP8X4),
-                    lhsT_scale=proj_scales[PHI][row_half][:, cols],
-                    rhs=proj_codes[THETA][col_half][:].bitcast(FP8X4),
-                    rhs_scale=proj_scales[THETA][col_half][:],
-                    start=True,
-                    stop=True,
-                )
-                nc.scalar.activation(
-                    out=r_half[row_half * TILES + k][col_half][:], in_=bank[:], func=ACT.Relu, scale=RESULT_SCALE
-                )
+        def rectify(lhs, q, n):
+            nc.scalar.activation(out=new_tile("term", q, n)[:], in_=banks["product", lhs, q, n][:], func=ACT.Relu)
 
-        def symmetrise(row_half, col_half):
-            for k in range(TILES):
-                i = row_half * TILES + k
-                bank = psum.tile([P, BANK], F32, name="bank", tag="bank")
-                for m in range(TILES):
+        def add_up(lhs, q, n):
+            nc.vector.scalar_tensor_tensor(
+                out=new_tile("sum", q, n)[:],
+                in0=banks["product", lhs, q, n][:],
+                scalar=0.0,
+                in1=tiles["term", q, n][:],
+                op0=ALU.max,
+                op1=ALU.add,
+            )
+
+        def scale(q, n, engine):
+            scaled = new_tile("scaled", q, n)
+            if engine is nc.scalar:
+                nc.scalar.activation(out=scaled[:], in_=tiles["sum", q, n][:], func=ACT.Copy, scale=RESULT_SCALE)
+            else:
+                engine.tensor_scalar(
+                    out=scaled[:],
+                    in0=tiles["sum", q, n][:],
+                    scalar1=RESULT_SCALE,
+                    scalar2=0.0,
+                    op0=ALU.mult,
+                    op1=ALU.add,
+                )
+            store(q, n, scaled)
+
+        def transpose_blocks(name, q, n):
+            bank = banks["mirror", q, n] = new_bank()
+            for k in range(2):
+                for m in range(2):
                     nc.tensor.transpose(
-                        bank[:, m * P : (m + 1) * P],
-                        r_half[col_half * TILES + m][row_half][:, k * P : (k + 1) * P],
+                        bank[:, k * Q + m * P : k * Q + (m + 1) * P],
+                        tiles[name, q, n][:, m * Q + k * P : m * Q + (k + 1) * P],
                         identity[:],
                     )
-                nc.vector.tensor_tensor(out=out_half[i][col_half][:], in0=bank[:], in1=r_half[i][col_half][:], op=ALU.add)
-                nc.sync.dma_start(
-                    out=result[i * P : (i + 1) * P, col_half * BANK : (col_half + 1) * BANK], in_=out_half[i][col_half][:]
+
+        def mirror(q, n, engine):
+            mirrored = new_tile("mirrored", q, n)
+            bank = banks["mirror", q, n]
+            if engine is nc.scalar:
+                nc.scalar.activation(out=mirrored[:], in_=bank[:], func=ACT.Copy, scale=RESULT_SCALE)
+            else:
+                nc.vector.tensor_scalar(
+                    out=mirrored[:], in0=bank[:], scalar1=RESULT_SCALE, scalar2=None, op0=ALU.mult
                 )
+            store(n, q, mirrored)
+
+        def rectify_diagonal(q):
+            nc.scalar.activation(
+                out=new_tile("term", q, q)[:], in_=banks["product", PHI, q, q][:], func=ACT.Relu, scale=RESULT_SCALE
+            )
+
+        def add_diagonal(q):
+            done = new_tile("scaled", q, q)
+            nc.vector.tensor_tensor(
+                out=done[:], in0=banks["mirror", q, q][:], in1=tiles["term", q, q][:], op=ALU.add
+            )
+            store(q, q, done)
 
         with tc.manual_schedule():
             make_identity(nc, identity[:])
             load_x(0)
-            load_x(1)
-            load_bias()
             load_weight(PHI)
-            load_x(2)
-            load_x(3)
+            load_bias()
             load_weight(THETA)
+            for q in range(1, QUARTERS):
+                load_x(q)
 
             transpose_x(0)
-            transpose_x(1)
+            regroup_x(0, nc.scalar)
+            regroup_weight(PHI, 0, nc.vector)
+            regroup_weight(PHI, 3, nc.scalar)
+            regroup_weight(PHI, 1, nc.vector)
+            quantise_weight(PHI, 0)
             quantise_x(0)
-            quantise_x(1)
-            quantise_weight(PHI)
-            transpose_x(2)
-            transpose_x(3)
-            quantise_x(2)
-            quantise_x(3)
-
+            regroup_weight(PHI, 2, nc.vector)
+            quantise_weight(PHI, 1)
+            regroup_weight(THETA, 3, nc.scalar)
+            regroup_weight(THETA, 2, nc.scalar)
+            quantise_weight(PHI, 2)
+            quantise_weight(PHI, 3)
+            transpose_x(1)
             project(PHI, 0)
-            quantise_weight(THETA)
-            quantise_projection(PHI, 0)
-            project(THETA, 0)
+            regroup_weight(THETA, 0, nc.vector)
+            regroup_weight(THETA, 1, nc.vector)
+            regroup_x(1, nc.scalar)
+            for t in range(PACK):
+                add_bias(PHI, 0, t)
+            for t in range(PACK):
+                quantise_weight(THETA, t)
+            project_words(THETA, 0)
+            quantise_x(1)
+            add_bias_words(THETA, 0, 0)
+            regroup(PHI, 0)
+            add_bias_words(THETA, 0, 1)
+            transpose_x(2)
             project(PHI, 1)
-            quantise_projection(THETA, 0)
-            quantise_projection(PHI, 1)
-            project(THETA, 1)
-
-            scores(0, 0)
-            scores(1, 0)
-            quantise_projection(THETA, 1)
-            symmetrise(0, 0)
-            scores(0, 1)
-            symmetrise(0, 1)
-            scores(1, 1)
-            symmetrise(1, 0)
-            symmetrise(1, 1)
+            project_words(THETA, 1)
+            regroup_x(2, nc.scalar)
+            for t in range(PACK):
+                add_bias(PHI, 1, t)
+            quantise(PHI, 0)
+            quantise(THETA, 0)
+            quantise_x(2)
+            transpose_x(3)
+            regroup_x(3, nc.scalar)
+            project(PHI, 2)
+            project(THETA, 2)
+            for t in range(PACK):
+                add_bias(PHI, 2, t)
+            product(PHI, THETA, 0, 0)
+            add_bias_words(THETA, 1, 0)
+            add_bias_words(THETA, 1, 1)
+            regroup(PHI, 1)
+            quantise(THETA, 1)
+            quantise(PHI, 1)
+            quantise_x(3)
+            rectify_diagonal(0)
+            for t in range(PACK):
+                add_bias(THETA, 2, t)
+            transpose_blocks("term", 0, 0)
+            product(PHI, THETA, 1, 0)
+            product(PHI, THETA, 1, 1)
+            product(THETA, PHI, 1, 0)
+            rectify(PHI, 1, 0)
+            rectify_diagonal(1)
+            project(PHI, 3)
+            regroup(PHI, 2)
+            add_diagonal(0)
+            regroup(THETA, 2)
+            transpose_blocks("term", 1, 1)
+            quantise(PHI, 2)
+            add_up(THETA, 1, 0)
+            quantise(THETA, 2)
+            for t in range(PACK):
+                add_bias(PHI, 3, t)
+            transpose_blocks("sum", 1, 0)
+            add_diagonal(1)
+            scale(1, 0, nc.vector)
+            mirror(1, 0, nc.scalar)
+            for n in range(2):
+                product(PHI, THETA, 2, n)
+                rectify(PHI, 2, n)
+                product(THETA, PHI, 2, n)
+            project(THETA, 3)
+            for t in range(PACK):
+                add_bias(THETA, 3, t)
+            product(PHI, THETA, 2, 2)
+            rectify_diagonal(2)
+            regroup(PHI, 3)
+            add_up(THETA, 2, 0)
+            transpose_blocks("sum", 2, 0)
+            quantise(PHI, 3)
+            add_up(THETA, 2, 1)
+            transpose_blocks("sum", 2, 1)
+            scale(2, 0, nc.vector)
+            regroup(THETA, 3)
+            scale(2, 1, nc.vector)
+            transpose_blocks("term", 2, 2)
+            mirror(2, 0, nc.scalar)
+            for n in range(2):
+                product(PHI, THETA, 3, n)
+            quantise(THETA, 3)
+            mirror(2, 1, nc.scalar)
+            add_diagonal(2)
+            for n in range(2):
+                rectify(PHI, 3, n)
+                product(THETA, PHI, 3, n)
+                add_up(THETA, 3, n)
+            product(PHI, THETA, 3, 2)
+            product(PHI, THETA, 3, 3)
+            product(THETA, PHI, 3, 2)
+            rectify(PHI, 3, 2)
+            rectify_diagonal(3)
+            scale(3, 0, nc.gpsimd)
+            scale(3, 1, nc.gpsimd)
+            for n in range(2):
+                transpose_blocks("sum", 3, n)
+            transpose_blocks("term", 3, 3)
+            add_up(THETA, 3, 2)
+            mirror(3, 0, nc.scalar)
+            mirror(3, 1, nc.scalar)
+            scale(3, 2, nc.vector)
+            transpose_blocks("sum", 3, 2)
+            add_diagonal(3)
+            mirror(3, 2, nc.scalar)

@@ -256,32 +256,43 @@ def tile_selfattention_pa_kernel(tc, audio_feature, W_phi, b_phi, W_theta, b_the
             )
             store(q, q, done)
 
+        warm_left = keep.tile([P, P], BF16)
+        warm_right = keep.tile([P, BANK], BF16)
+
+        def keep_warm(count):
+            for n in range(count):
+                nc.tensor.matmul(new_bank()[:], lhsT=warm_left[:], rhs=warm_right[:], start=True, stop=True)
+
         with tc.manual_schedule():
+            nc.vector.memset(warm_left[:], 0.0)
+            nc.vector.memset(warm_right[:], 0.0)
             make_identity(nc, identity[:])
-            load_x(0)
             load_weight(PHI)
-            load_bias()
+            load_x(0)
             load_weight(THETA)
+            load_bias()
             for q in range(1, QUARTERS):
                 load_x(q)
 
+            keep_warm(4)
             transpose_x(0)
-            regroup_x(0, nc.scalar)
             regroup_weight(PHI, 0, nc.vector)
             regroup_weight(PHI, 3, nc.scalar)
             regroup_weight(PHI, 1, nc.vector)
             quantise_weight(PHI, 0)
-            quantise_x(0)
             regroup_weight(PHI, 2, nc.vector)
             quantise_weight(PHI, 1)
-            regroup_weight(THETA, 3, nc.scalar)
-            regroup_weight(THETA, 2, nc.scalar)
             quantise_weight(PHI, 2)
             quantise_weight(PHI, 3)
+            regroup_x(0, nc.scalar)
+            keep_warm(2)
+            regroup_weight(THETA, 0, nc.vector)
+            regroup_weight(THETA, 3, nc.scalar)
+            quantise_x(0)
             transpose_x(1)
             project(PHI, 0)
-            regroup_weight(THETA, 0, nc.vector)
             regroup_weight(THETA, 1, nc.vector)
+            regroup_weight(THETA, 2, nc.vector)
             regroup_x(1, nc.scalar)
             for t in range(PACK):
                 add_bias(PHI, 0, t)
@@ -290,16 +301,16 @@ def tile_selfattention_pa_kernel(tc, audio_feature, W_phi, b_phi, W_theta, b_the
             project_words(THETA, 0)
             quantise_x(1)
             add_bias_words(THETA, 0, 0)
-            regroup(PHI, 0)
             add_bias_words(THETA, 0, 1)
+            regroup(PHI, 0)
             transpose_x(2)
             project(PHI, 1)
             project_words(THETA, 1)
             regroup_x(2, nc.scalar)
             for t in range(PACK):
                 add_bias(PHI, 1, t)
-            quantise(PHI, 0)
             quantise(THETA, 0)
+            quantise(PHI, 0)
             quantise_x(2)
             transpose_x(3)
             regroup_x(3, nc.scalar)
@@ -324,62 +335,66 @@ def tile_selfattention_pa_kernel(tc, audio_feature, W_phi, b_phi, W_theta, b_the
             rectify(PHI, 1, 0)
             rectify_diagonal(1)
             project(PHI, 3)
+            project(THETA, 3)
             regroup(PHI, 2)
             add_diagonal(0)
             regroup(THETA, 2)
+            for t in range(PACK):
+                add_bias(PHI, 3, t)
             transpose_blocks("term", 1, 1)
             quantise(PHI, 2)
             add_up(THETA, 1, 0)
             quantise(THETA, 2)
             for t in range(PACK):
-                add_bias(PHI, 3, t)
-            transpose_blocks("sum", 1, 0)
-            add_diagonal(1)
-            scale(1, 0, nc.vector)
-            mirror(1, 0, nc.scalar)
-            for n in range(2):
-                product(PHI, THETA, 2, n)
-                rectify(PHI, 2, n)
-                product(THETA, PHI, 2, n)
-            project(THETA, 3)
-            for t in range(PACK):
                 add_bias(THETA, 3, t)
+            transpose_blocks("sum", 1, 0)
+            scale(1, 0, nc.vector)
+            add_diagonal(1)
+            mirror(1, 0, nc.scalar)
+            regroup(PHI, 3)
+            product(PHI, THETA, 2, 0)
+            rectify(PHI, 2, 0)
+            product(THETA, PHI, 2, 0)
+            regroup(THETA, 3)
+            product(PHI, THETA, 2, 1)
+            rectify(PHI, 2, 1)
+            product(THETA, PHI, 2, 1)
+            quantise(PHI, 3)
+            add_up(THETA, 2, 0)
+            quantise(THETA, 3)
+            scale(2, 0, nc.vector)
             product(PHI, THETA, 2, 2)
             rectify_diagonal(2)
-            regroup(PHI, 3)
-            add_up(THETA, 2, 0)
+            product(PHI, THETA, 3, 0)
+            rectify(PHI, 3, 0)
+            product(PHI, THETA, 3, 1)
             transpose_blocks("sum", 2, 0)
-            quantise(PHI, 3)
+            product(THETA, PHI, 3, 0)
+            mirror(2, 0, nc.scalar)
             add_up(THETA, 2, 1)
-            transpose_blocks("sum", 2, 1)
-            scale(2, 0, nc.vector)
-            regroup(THETA, 3)
             scale(2, 1, nc.vector)
             transpose_blocks("term", 2, 2)
-            mirror(2, 0, nc.scalar)
-            for n in range(2):
-                product(PHI, THETA, 3, n)
-            quantise(THETA, 3)
+            transpose_blocks("sum", 2, 1)
+            rectify(PHI, 3, 1)
+            product(THETA, PHI, 3, 1)
             mirror(2, 1, nc.scalar)
+            add_up(THETA, 3, 0)
+            scale(3, 0, nc.vector)
             add_diagonal(2)
-            for n in range(2):
-                rectify(PHI, 3, n)
-                product(THETA, PHI, 3, n)
-                add_up(THETA, 3, n)
             product(PHI, THETA, 3, 2)
-            product(PHI, THETA, 3, 3)
-            product(THETA, PHI, 3, 2)
             rectify(PHI, 3, 2)
+            product(PHI, THETA, 3, 3)
             rectify_diagonal(3)
-            scale(3, 0, nc.gpsimd)
-            scale(3, 1, nc.gpsimd)
-            for n in range(2):
-                transpose_blocks("sum", 3, n)
+            product(THETA, PHI, 3, 2)
+            transpose_blocks("sum", 3, 0)
+            add_up(THETA, 3, 1)
+            scale(3, 1, nc.vector)
+            mirror(3, 0, nc.scalar)
+            transpose_blocks("sum", 3, 1)
             transpose_blocks("term", 3, 3)
             add_up(THETA, 3, 2)
-            mirror(3, 0, nc.scalar)
-            mirror(3, 1, nc.scalar)
             scale(3, 2, nc.vector)
+            mirror(3, 1, nc.scalar)
             transpose_blocks("sum", 3, 2)
             add_diagonal(3)
             mirror(3, 2, nc.scalar)

@@ -69,7 +69,7 @@ def tile_selfattention_pa_kernel(tc, audio_feature, W_phi, b_phi, W_theta, b_the
 
         def load_bias():
             for o in (PHI, THETA):
-                nc.sync.dma_start(out=bias_cols[o][:], in_=biases[o].rearrange("(p j) -> p j", j=PACK))
+                nc.scalar.dma_start(out=bias_cols[o][:], in_=biases[o].rearrange("(p j) -> p j", j=PACK))
 
         def copy(engine, target, source):
             if engine is nc.scalar:
@@ -267,10 +267,10 @@ def tile_selfattention_pa_kernel(tc, audio_feature, W_phi, b_phi, W_theta, b_the
             nc.vector.memset(warm_left[:], 0.0)
             nc.vector.memset(warm_right[:], 0.0)
             make_identity(nc, identity[:])
+            load_bias()
             load_weight(PHI)
             load_x(0)
             load_weight(THETA)
-            load_bias()
             for q in range(1, QUARTERS):
                 load_x(q)
 
@@ -372,15 +372,15 @@ def tile_selfattention_pa_kernel(tc, audio_feature, W_phi, b_phi, W_theta, b_the
             product(THETA, PHI, 3, 0)
             mirror(2, 0, nc.scalar)
             add_up(THETA, 2, 1)
+            add_up(THETA, 3, 0)
             scale(2, 1, nc.vector)
             transpose_blocks("term", 2, 2)
             transpose_blocks("sum", 2, 1)
             rectify(PHI, 3, 1)
             product(THETA, PHI, 3, 1)
             mirror(2, 1, nc.scalar)
-            add_up(THETA, 3, 0)
-            scale(3, 0, nc.vector)
             add_diagonal(2)
+            scale(3, 0, nc.vector)
             product(PHI, THETA, 3, 2)
             rectify(PHI, 3, 2)
             product(PHI, THETA, 3, 3)
@@ -388,13 +388,13 @@ def tile_selfattention_pa_kernel(tc, audio_feature, W_phi, b_phi, W_theta, b_the
             product(THETA, PHI, 3, 2)
             transpose_blocks("sum", 3, 0)
             add_up(THETA, 3, 1)
-            scale(3, 1, nc.vector)
             mirror(3, 0, nc.scalar)
+            add_up(THETA, 3, 2)
+            scale(3, 1, nc.vector)
             transpose_blocks("sum", 3, 1)
             transpose_blocks("term", 3, 3)
-            add_up(THETA, 3, 2)
-            scale(3, 2, nc.vector)
             mirror(3, 1, nc.scalar)
-            transpose_blocks("sum", 3, 2)
             add_diagonal(3)
+            scale(3, 2, nc.vector)
+            transpose_blocks("sum", 3, 2)
             mirror(3, 2, nc.scalar)

@@ -51,9 +51,9 @@ def tile_selfattention_pa_kernel(tc, audio_feature, W_phi, b_phi, W_theta, b_the
         w_scales = [keep.tile([P, H], U8, name="w_scales%d" % o, align_bytes=64) for o in (PHI, THETA)]
 
         proj_planes = [per_quarter("proj_planes%d_" % o, PACK * Q, BF16) for o in (PHI, THETA)]
-        proj_grouped = [per_quarter("proj_grouped%d_" % o, Q * PACK, BF16) for o in (PHI, THETA)]
-        proj_codes = [per_quarter("proj_codes%d_" % o, Q, U32) for o in (PHI, THETA)]
-        proj_scales = [per_quarter("proj_scales%d_" % o, Q, U8) for o in (PHI, THETA)]
+        proj_grouped = per_quarter("proj_grouped", 2 * Q * PACK, BF16)
+        proj_codes = per_quarter("proj_codes", 2 * Q, U32)
+        proj_scales = per_quarter("proj_scales", 2 * Q, U8)
 
         def load_x(q):
             nc.sync.dma_start(
@@ -80,19 +80,20 @@ def tile_selfattention_pa_kernel(tc, audio_feature, W_phi, b_phi, W_theta, b_the
         def new_bank():
             return psum.tile([P, BANK], F32, name="bank", tag="bank")
 
-        def regroup_weight(o, t, engine):
+        def regroup_weight(o, half, engine):
+            ts = slice(2 * half, 2 * half + 2)
             copy(
                 engine,
-                w_grouped[o][:].rearrange("p (t m j) -> p t m j", t=PACK, j=PACK)[:, t],
-                w_raw[o][:].rearrange("p (j m t) -> p t m j", j=PACK, t=PACK)[:, t],
+                w_grouped[o][:].rearrange("p (t m j) -> p t m j", t=PACK, j=PACK)[:, ts],
+                w_raw[o][:].rearrange("p (j m t) -> p t m j", j=PACK, t=PACK)[:, ts],
             )
 
-        def quantise_weight(o, t):
-            cols = slice(t * P, (t + 1) * P)
+        def quantise_weight(o, half):
+            cols = slice(half * H // 2, (half + 1) * H // 2)
             nc.vector.quantize_mx(
                 out=w_codes[o][:, cols].bitcast(FP8X4),
                 scales=w_scales[o][:, cols],
-                in_=w_grouped[o][:, t * P * PACK : (t + 1) * P * PACK],
+                in_=w_grouped[o][:, half * H // 2 * PACK : (half + 1) * H // 2 * PACK],
             )
 
         banks = {}
@@ -146,7 +147,7 @@ def tile_selfattention_pa_kernel(tc, audio_feature, W_phi, b_phi, W_theta, b_the
 
         def regroup(o, q):
             nc.vector.tensor_copy(
-                out=proj_grouped[o][q][:].rearrange("p (c i t) -> p c t i", i=4, t=PACK),
+                out=proj_grouped[q][:, o * Q * PACK : (o + 1) * Q * PACK].rearrange("p (c i t) -> p c t i", i=4, t=PACK),
                 in_=proj_planes[o][q][:].rearrange("p (t c i) -> p c t i", i=4, t=PACK),
             )
 
@@ -158,27 +159,31 @@ def tile_selfattention_pa_kernel(tc, audio_feature, W_phi, b_phi, W_theta, b_the
 
         def add_bias_words(o, q, k):
             nc.vector.tensor_tensor(
-                out=proj_grouped[o][q][:, k * BANK : (k + 1) * BANK].rearrange("p (c t) -> p c t", t=PACK),
+                out=proj_grouped[q][:, (2 * o + k) * BANK : (2 * o + k + 1) * BANK].rearrange("p (c t) -> p c t", t=PACK),
                 in0=banks["words", o, q, k][:].rearrange("p (t c) -> p c t", t=PACK),
                 in1=bias_cols[o][:].unsqueeze(1).to_broadcast([P, P, PACK]),
                 op=ALU.add,
             )
 
-        def quantise(o, q):
+        def quantise(q, first=PHI, last=THETA):
+            cols = slice(first * Q, (last + 1) * Q)
             nc.vector.quantize_mx(
-                out=proj_codes[o][q][:].bitcast(FP8X4), scales=proj_scales[o][q][:], in_=proj_grouped[o][q][:]
+                out=proj_codes[q][:, cols].bitcast(FP8X4),
+                scales=proj_scales[q][:, cols],
+                in_=proj_grouped[q][:, first * Q * PACK : (last + 1) * Q * PACK],
             )
 
         def product(lhs, rhs, q, n):
             bank = banks["product", lhs, q, n] = new_bank()
             for k in range(2):
-                rows = slice(k * P, (k + 1) * P)
+                rows = slice(lhs * Q + k * P, lhs * Q + (k + 1) * P)
+                cols = slice(rhs * Q, (rhs + 1) * Q)
                 nc.tensor.matmul_mx(
                     out=bank[:, k * Q : (k + 1) * Q],
-                    lhsT=proj_codes[lhs][q][:, rows].bitcast(FP8X4),
-                    lhsT_scale=proj_scales[lhs][q][:, rows],
-                    rhs=proj_codes[rhs][n][:].bitcast(FP8X4),
-                    rhs_scale=proj_scales[rhs][n][:],
+                    lhsT=proj_codes[q][:, rows].bitcast(FP8X4),
+                    lhsT_scale=proj_scales[q][:, rows],
+                    rhs=proj_codes[n][:, cols].bitcast(FP8X4),
+                    rhs_scale=proj_scales[n][:, cols],
                     start=True,
                     stop=True,
                 )
@@ -277,27 +282,21 @@ def tile_selfattention_pa_kernel(tc, audio_feature, W_phi, b_phi, W_theta, b_the
             keep_warm(4)
             transpose_x(0)
             regroup_weight(PHI, 0, nc.vector)
-            regroup_weight(PHI, 3, nc.scalar)
-            regroup_weight(PHI, 1, nc.vector)
+            regroup_weight(PHI, 1, nc.scalar)
             quantise_weight(PHI, 0)
-            regroup_weight(PHI, 2, nc.vector)
-            quantise_weight(PHI, 1)
-            quantise_weight(PHI, 2)
-            quantise_weight(PHI, 3)
             regroup_x(0, nc.scalar)
             keep_warm(2)
+            quantise_weight(PHI, 1)
             regroup_weight(THETA, 0, nc.vector)
-            regroup_weight(THETA, 3, nc.scalar)
+            regroup_weight(THETA, 1, nc.scalar)
             quantise_x(0)
             transpose_x(1)
             project(PHI, 0)
-            regroup_weight(THETA, 1, nc.vector)
-            regroup_weight(THETA, 2, nc.vector)
+            quantise_weight(THETA, 0)
             regroup_x(1, nc.scalar)
             for t in range(PACK):
                 add_bias(PHI, 0, t)
-            for t in range(PACK):
-                quantise_weight(THETA, t)
+            quantise_weight(THETA, 1)
             project_words(THETA, 0)
             quantise_x(1)
             add_bias_words(THETA, 0, 0)
@@ -309,92 +308,84 @@ def tile_selfattention_pa_kernel(tc, audio_feature, W_phi, b_phi, W_theta, b_the
             regroup_x(2, nc.scalar)
             for t in range(PACK):
                 add_bias(PHI, 1, t)
-            quantise(THETA, 0)
-            quantise(PHI, 0)
             quantise_x(2)
+            quantise(0)
             transpose_x(3)
             regroup_x(3, nc.scalar)
             project(PHI, 2)
-            project(THETA, 2)
+            project_words(THETA, 2)
             for t in range(PACK):
                 add_bias(PHI, 2, t)
             product(PHI, THETA, 0, 0)
             add_bias_words(THETA, 1, 0)
             add_bias_words(THETA, 1, 1)
             regroup(PHI, 1)
-            quantise(THETA, 1)
-            quantise(PHI, 1)
             quantise_x(3)
+            quantise(1)
             rectify_diagonal(0)
+            project(PHI, 3)
             for t in range(PACK):
-                add_bias(THETA, 2, t)
+                add_bias(PHI, 3, t)
+            add_bias_words(THETA, 2, 0)
             transpose_blocks("term", 0, 0)
+            add_bias_words(THETA, 2, 1)
             product(PHI, THETA, 1, 0)
             product(PHI, THETA, 1, 1)
             product(THETA, PHI, 1, 0)
             rectify(PHI, 1, 0)
             rectify_diagonal(1)
-            project(PHI, 3)
             project(THETA, 3)
             regroup(PHI, 2)
             add_diagonal(0)
-            regroup(THETA, 2)
-            for t in range(PACK):
-                add_bias(PHI, 3, t)
-            transpose_blocks("term", 1, 1)
-            quantise(PHI, 2)
-            add_up(THETA, 1, 0)
-            quantise(THETA, 2)
             for t in range(PACK):
                 add_bias(THETA, 3, t)
+            add_up(THETA, 1, 0)
+            transpose_blocks("term", 1, 1)
+            quantise(2)
             transpose_blocks("sum", 1, 0)
             scale(1, 0, nc.vector)
             add_diagonal(1)
             mirror(1, 0, nc.scalar)
-            regroup(PHI, 3)
-            product(PHI, THETA, 2, 0)
-            rectify(PHI, 2, 0)
-            product(THETA, PHI, 2, 0)
-            regroup(THETA, 3)
-            product(PHI, THETA, 2, 1)
-            rectify(PHI, 2, 1)
-            product(THETA, PHI, 2, 1)
-            quantise(PHI, 3)
-            add_up(THETA, 2, 0)
-            quantise(THETA, 3)
-            scale(2, 0, nc.vector)
+            for n in range(2):
+                product(PHI, THETA, 2, n)
+                rectify(PHI, 2, n)
+                product(THETA, PHI, 2, n)
             product(PHI, THETA, 2, 2)
             rectify_diagonal(2)
+            regroup(PHI, 3)
+            add_up(THETA, 2, 0)
+            quantise(3, PHI, PHI)
+            scale(2, 0, nc.vector)
+            transpose_blocks("sum", 2, 0)
+            mirror(2, 0, nc.scalar)
             product(PHI, THETA, 3, 0)
             rectify(PHI, 3, 0)
-            product(PHI, THETA, 3, 1)
-            transpose_blocks("sum", 2, 0)
-            product(THETA, PHI, 3, 0)
-            mirror(2, 0, nc.scalar)
             add_up(THETA, 2, 1)
-            add_up(THETA, 3, 0)
+            regroup(THETA, 3)
             scale(2, 1, nc.vector)
-            transpose_blocks("term", 2, 2)
             transpose_blocks("sum", 2, 1)
-            rectify(PHI, 3, 1)
-            product(THETA, PHI, 3, 1)
+            transpose_blocks("term", 2, 2)
             mirror(2, 1, nc.scalar)
+            quantise(3, THETA, THETA)
+            for n in range(1, 3):
+                product(PHI, THETA, 3, n)
+                rectify(PHI, 3, n)
             add_diagonal(2)
-            scale(3, 0, nc.vector)
-            product(PHI, THETA, 3, 2)
-            rectify(PHI, 3, 2)
+            for n in range(3):
+                product(THETA, PHI, 3, n)
             product(PHI, THETA, 3, 3)
             rectify_diagonal(3)
-            product(THETA, PHI, 3, 2)
-            transpose_blocks("sum", 3, 0)
+            add_up(THETA, 3, 0)
             add_up(THETA, 3, 1)
+            scale(3, 0, nc.vector)
+            transpose_blocks("sum", 3, 0)
             mirror(3, 0, nc.scalar)
             add_up(THETA, 3, 2)
             scale(3, 1, nc.vector)
             transpose_blocks("sum", 3, 1)
-            transpose_blocks("term", 3, 3)
             mirror(3, 1, nc.scalar)
-            add_diagonal(3)
+            transpose_blocks("term", 3, 3)
             scale(3, 2, nc.vector)
             transpose_blocks("sum", 3, 2)
             mirror(3, 2, nc.scalar)
+            add_diagonal(3)

@@ -355,7 +355,7 @@ def tile_selfattention_pa_kernel(tc, audio_feature, W_phi, b_phi, W_theta, b_the
             regroup(PHI, 3)
             add_up(THETA, 2, 0)
             quantise(3, PHI, PHI)
-            scale(2, 0, nc.vector)
+            scale(2, 0, nc.scalar)
             transpose_blocks("sum", 2, 0)
             mirror(2, 0, nc.scalar)
             product(PHI, THETA, 3, 0)

@@ -218,13 +218,8 @@ def tile_selfattention_pa_kernel(tc, audio_feature, W_phi, b_phi, W_theta, b_the
             if engine is nc.scalar:
                 nc.scalar.activation(out=scaled[:], in_=tiles["sum", q, n][:], func=ACT.Copy, scale=RESULT_SCALE)
             else:
-                engine.tensor_scalar(
-                    out=scaled[:],
-                    in0=tiles["sum", q, n][:],
-                    scalar1=RESULT_SCALE,
-                    scalar2=0.0,
-                    op0=ALU.mult,
-                    op1=ALU.add,
+                nc.vector.tensor_scalar(
+                    out=scaled[:], in0=tiles["sum", q, n][:], scalar1=RESULT_SCALE, scalar2=None, op0=ALU.mult
                 )
             store(q, n, scaled)
 

@@ -319,32 +319,36 @@ def tile_selfattention_pa_kernel(tc, audio_feature, W_phi, b_phi, W_theta, b_the
             quantise(1)
             rectify_diagonal(0)
             project(PHI, 3)
-            for t in range(PACK):
+            for t in range(2):
                 add_bias(PHI, 3, t)
             add_bias_words(THETA, 2, 0)
-            transpose_blocks("term", 0, 0)
             add_bias_words(THETA, 2, 1)
             product(PHI, THETA, 1, 0)
             product(PHI, THETA, 1, 1)
             product(THETA, PHI, 1, 0)
             rectify(PHI, 1, 0)
+            for t in range(2, PACK):
+                add_bias(PHI, 3, t)
             rectify_diagonal(1)
             project(THETA, 3)
+            transpose_blocks("term", 0, 0)
             regroup(PHI, 2)
-            add_diagonal(0)
             for t in range(PACK):
                 add_bias(THETA, 3, t)
             add_up(THETA, 1, 0)
-            transpose_blocks("term", 1, 1)
             quantise(2)
+            add_diagonal(0)
             transpose_blocks("sum", 1, 0)
+            transpose_blocks("term", 1, 1)
+            product(PHI, THETA, 2, 0)
+            product(THETA, PHI, 2, 0)
+            rectify(PHI, 2, 0)
             scale(1, 0, nc.vector)
             add_diagonal(1)
             mirror(1, 0, nc.scalar)
-            for n in range(2):
-                product(PHI, THETA, 2, n)
-                rectify(PHI, 2, n)
-                product(THETA, PHI, 2, n)
+            product(PHI, THETA, 2, 1)
+            rectify(PHI, 2, 1)
+            product(THETA, PHI, 2, 1)
             product(PHI, THETA, 2, 2)
             rectify_diagonal(2)
             regroup(PHI, 3)

@@ -194,8 +194,8 @@ def tile_selfattention_pa_kernel(tc, audio_feature, W_phi, b_phi, W_theta, b_the
             tiles[name, q, n] = keep.tile([P, BANK], F32, name="%s_%d_%d" % (name, q, n))
             return tiles[name, q, n]
 
-        def store(q, n, tile):
-            nc.sync.dma_start(
+        def store(q, n, tile, queue=nc.sync):
+            queue.dma_start(
                 out=result[q * Q : (q + 1) * Q, n * Q : (n + 1) * Q].rearrange("(k p) c -> p k c", p=P),
                 in_=tile[:].rearrange("p (k c) -> p k c", k=2),
             )
@@ -242,7 +242,7 @@ def tile_selfattention_pa_kernel(tc, audio_feature, W_phi, b_phi, W_theta, b_the
                 nc.vector.tensor_scalar(
                     out=mirrored[:], in0=bank[:], scalar1=RESULT_SCALE, scalar2=None, op0=ALU.mult
                 )
-            store(n, q, mirrored)
+            store(n, q, mirrored, nc.scalar if q == QUARTERS - 1 else nc.sync)
 
         def rectify_diagonal(q):
             nc.scalar.activation(

import math

import concourse.mybir as mybir
from concourse.masks import make_identity

F32 = mybir.dt.float32
BF16 = mybir.dt.bfloat16
U32 = mybir.dt.uint32
U8 = mybir.dt.uint8
FP8X4 = mybir.dt.float8_e4m3fn_x4
ACT = mybir.ActivationFunctionType
ALU = mybir.AluOpType

P = 128
PACK = 4
S = 1024
D = 512
H = 512
BANK = 512
Q = 2 * P
QUARTERS = S // Q
PHI = 0
THETA = 1
RESULT_SCALE = 0.5 / math.sqrt(D)

FLOPS = 2 * (2 * S * D * H) + 2 * S * S * H


def tile_selfattention_pa_kernel(tc, audio_feature, W_phi, b_phi, W_theta, b_theta, out):
    nc = tc.nc
    x = audio_feature.flatten_outer_dims()
    result = out.flatten_outer_dims()
    weights = (W_phi, W_theta)
    biases = (b_phi, b_theta)

    with tc.tile_pool(name="keep", bufs=1) as keep, tc.psum_pool(name="psum", bufs=8) as psum:
        def per_quarter(name, width, dtype):
            return [keep.tile([P, width], dtype, name="%s%d" % (name, q), align_bytes=64) for q in range(QUARTERS)]

        identity = keep.tile([P, P], F32)
        bias_cols = [keep.tile([P, PACK], BF16, name="bias_cols%d" % o) for o in (PHI, THETA)]

        x_raw = per_quarter("x_raw", 2 * D, BF16)
        x_grouped = per_quarter("x_grouped", Q * PACK, BF16)
        x_codes = per_quarter("x_codes", Q, U32)
        x_scales = per_quarter("x_scales", Q, U8)

        w_raw = [keep.tile([P, PACK * H], BF16, name="w_raw%d" % o) for o in (PHI, THETA)]
        w_grouped = [keep.tile([P, H * PACK], BF16, name="w_grouped%d" % o, align_bytes=64) for o in (PHI, THETA)]
        w_codes = [keep.tile([P, H], U32, name="w_codes%d" % o, align_bytes=64) for o in (PHI, THETA)]
        w_scales = [keep.tile([P, H], U8, name="w_scales%d" % o, align_bytes=64) for o in (PHI, THETA)]

        proj_planes = [per_quarter("proj_planes%d_" % o, PACK * Q, BF16) for o in (PHI, THETA)]
        proj_grouped = per_quarter("proj_grouped", 2 * Q * PACK, BF16)
        proj_codes = per_quarter("proj_codes", 2 * Q, U32)
        proj_scales = per_quarter("proj_scales", 2 * Q, U8)

        def load_x(q):
            nc.sync.dma_start(
                out=x_raw[q][:].rearrange("p (t d) -> p t d", t=2),
                in_=x[q * Q : (q + 1) * Q, :].rearrange("(t p) d -> p t d", p=P),
            )

        def load_weight(o):
            nc.sync.dma_start(
                out=w_raw[o][:].rearrange("p (j h) -> p j h", j=PACK),
                in_=weights[o].rearrange("(p j) h -> p j h", j=PACK),
            )

        def load_bias():
            for o in (PHI, THETA):
                nc.scalar.dma_start(out=bias_cols[o][:], in_=biases[o].rearrange("(p j) -> p j", j=PACK))

        def copy(engine, target, source):
            if engine is nc.scalar:
                nc.scalar.copy(out=target, in_=source)
            else:
                nc.vector.tensor_copy(out=target, in_=source)

        def new_bank():
            return psum.tile([P, BANK], F32, name="bank", tag="bank")

        def regroup_weight(o, half, engine):
            ts = slice(2 * half, 2 * half + 2)
            copy(
                engine,
                w_grouped[o][:].rearrange("p (t m j) -> p t m j", t=PACK, j=PACK)[:, ts],
                w_raw[o][:].rearrange("p (j m t) -> p t m j", j=PACK, t=PACK)[:, ts],
            )

        def quantise_weight(o, half):
            cols = slice(half * H // 2, (half + 1) * H // 2)
            nc.vector.quantize_mx(
                out=w_codes[o][:, cols].bitcast(FP8X4),
                scales=w_scales[o][:, cols],
                in_=w_grouped[o][:, half * H // 2 * PACK : (half + 1) * H // 2 * PACK],
            )

        banks = {}

        def transpose_x(q):
            words = x_raw[q][:].bitcast(F32)
            bank = banks["x", q] = new_bank()
            for t in range(2):
                for u in range(2):
                    tu = 2 * t + u
                    nc.tensor.transpose(
                        bank[:, tu * P : (tu + 1) * P], words[:, 2 * P * t + u : 2 * P * (t + 1) : 2], identity[:]
                    )

        def regroup_x(q, engine):
            copy(
                engine,
                x_grouped[q][:].bitcast(F32).rearrange("p (t s u) -> p t s u", t=2, u=2),
                banks["x", q][:].rearrange("p (t u s) -> p t s u", t=2, u=2),
            )

        def quantise_x(q):
            nc.vector.quantize_mx(out=x_codes[q][:].bitcast(FP8X4), scales=x_scales[q][:], in_=x_grouped[q][:])

        def project_part(o, q, t, positions, part):
            nc.tensor.matmul_mx(
                out=part,
                lhsT=w_codes[o][:, t * P : (t + 1) * P].bitcast(FP8X4),
                lhsT_scale=w_scales[o][:, t * P : (t + 1) * P],
                rhs=x_codes[q][:, positions].bitcast(FP8X4),
                rhs_scale=x_scales[q][:, positions],
                start=True,
                stop=True,
            )

        def project(o, q):
            for t in range(PACK):
                if t % 2 == 0:
                    bank = new_bank()
                banks["plane", o, q, t] = bank[:, t % 2 * Q : (t % 2 + 1) * Q]
                project_part(o, q, t, slice(0, Q), banks["plane", o, q, t])

        def add_bias(o, q, t):
            nc.scalar.activation(
                out=proj_planes[o][q][:, t * Q : (t + 1) * Q],
                in_=banks["plane", o, q, t],
                func=ACT.Identity,
                bias=bias_cols[o][:, t : t + 1],
                scale=1.0,
            )

        def regroup(o, q):
            nc.vector.tensor_copy(
                out=proj_grouped[q][:, o * Q * PACK : (o + 1) * Q * PACK].rearrange("p (c i t) -> p c t i", i=4, t=PACK),
                in_=proj_planes[o][q][:].rearrange("p (t c i) -> p c t i", i=4, t=PACK),
            )

        def project_words(o, q):
            for k in range(2):
                bank = banks["words", o, q, k] = new_bank()
                for t in range(PACK):
                    project_part(o, q, t, slice(k * P, (k + 1) * P), bank[:, t * P : (t + 1) * P])

        def add_bias_words(o, q, k):
            nc.vector.tensor_tensor(
                out=proj_grouped[q][:, (2 * o + k) * BANK : (2 * o + k + 1) * BANK].rearrange("p (c t) -> p c t", t=PACK),
                in0=banks["words", o, q, k][:].rearrange("p (t c) -> p c t", t=PACK),
                in1=bias_cols[o][:].unsqueeze(1).to_broadcast([P, P, PACK]),
                op=ALU.add,
            )

        def quantise(q, first=PHI, last=THETA):
            cols = slice(first * Q, (last + 1) * Q)
            nc.vector.quantize_mx(
                out=proj_codes[q][:, cols].bitcast(FP8X4),
                scales=proj_scales[q][:, cols],
                in_=proj_grouped[q][:, first * Q * PACK : (last + 1) * Q * PACK],
            )

        def product(lhs, rhs, q, n):
            bank = banks["product", lhs, q, n] = new_bank()
            for k in range(2):
                rows = slice(lhs * Q + k * P, lhs * Q + (k + 1) * P)
                cols = slice(rhs * Q, (rhs + 1) * Q)
                nc.tensor.matmul_mx(
                    out=bank[:, k * Q : (k + 1) * Q],
                    lhsT=proj_codes[q][:, rows].bitcast(FP8X4),
                    lhsT_scale=proj_scales[q][:, rows],
                    rhs=proj_codes[n][:, cols].bitcast(FP8X4),
                    rhs_scale=proj_scales[n][:, cols],
                    start=True,
                    stop=True,
                )

        tiles = {}

        def new_tile(name, q, n):
            tiles[name, q, n] = keep.tile([P, BANK], F32, name="%s_%d_%d" % (name, q, n))
            return tiles[name, q, n]

        def store(q, n, tile, queue=nc.sync):
            queue.dma_start(
                out=result[q * Q : (q + 1) * Q, n * Q : (n + 1) * Q].rearrange("(k p) c -> p k c", p=P),
                in_=tile[:].rearrange("p (k c) -> p k c", k=2),
            )

        def rectify(lhs, q, n):
            nc.scalar.activation(out=new_tile("term", q, n)[:], in_=banks["product", lhs, q, n][:], func=ACT.Relu)

        def add_up(lhs, q, n):
            nc.vector.scalar_tensor_tensor(
                out=new_tile("sum", q, n)[:],
                in0=banks["product", lhs, q, n][:],
                scalar=0.0,
                in1=tiles["term", q, n][:],
                op0=ALU.max,
                op1=ALU.add,
            )

        def scale(q, n, engine):
            scaled = new_tile("scaled", q, n)
            if engine is nc.scalar:
                nc.scalar.activation(out=scaled[:], in_=tiles["sum", q, n][:], func=ACT.Copy, scale=RESULT_SCALE)
            else:
                nc.vector.tensor_scalar(
                    out=scaled[:], in0=tiles["sum", q, n][:], scalar1=RESULT_SCALE, scalar2=None, op0=ALU.mult
                )
            store(q, n, scaled)

        def transpose_blocks(name, q, n):
            bank = banks["mirror", q, n] = new_bank()
            for k in range(2):
                for m in range(2):
                    nc.tensor.transpose(
                        bank[:, k * Q + m * P : k * Q + (m + 1) * P],
                        tiles[name, q, n][:, m * Q + k * P : m * Q + (k + 1) * P],
                        identity[:],
                    )

        def mirror(q, n, engine):
            mirrored = new_tile("mirrored", q, n)
            bank = banks["mirror", q, n]
            if engine is nc.scalar:
                nc.scalar.activation(out=mirrored[:], in_=bank[:], func=ACT.Copy, scale=RESULT_SCALE)
            else:
                nc.vector.tensor_scalar(
                    out=mirrored[:], in0=bank[:], scalar1=RESULT_SCALE, scalar2=None, op0=ALU.mult
                )
            store(n, q, mirrored, nc.scalar if q == QUARTERS - 1 else nc.sync)

        def rectify_diagonal(q):
            nc.scalar.activation(
                out=new_tile("term", q, q)[:], in_=banks["product", PHI, q, q][:], func=ACT.Relu, scale=RESULT_SCALE
            )

        def add_diagonal(q):
            done = new_tile("scaled", q, q)
            nc.vector.tensor_tensor(
                out=done[:], in0=banks["mirror", q, q][:], in1=tiles["term", q, q][:], op=ALU.add
            )
            store(q, q, done)

        warm_left = keep.tile([P, P], BF16)
        warm_right = keep.tile([P, BANK], BF16)

        def keep_warm(count):
            for n in range(count):
                nc.tensor.matmul(new_bank()[:], lhsT=warm_left[:], rhs=warm_right[:], start=True, stop=True)

        with tc.manual_schedule():
            nc.vector.memset(warm_left[:], 0.0)
            nc.vector.memset(warm_right[:], 0.0)
            make_identity(nc, identity[:])
            load_bias()
            load_weight(PHI)
            load_x(0)
            load_weight(THETA)
            for q in range(1, QUARTERS):
                load_x(q)

            keep_warm(4)
            transpose_x(0)
            regroup_weight(PHI, 0, nc.vector)
            regroup_weight(PHI, 1, nc.scalar)
            quantise_weight(PHI, 0)
            regroup_x(0, nc.scalar)
            keep_warm(2)
            quantise_weight(PHI, 1)
            regroup_weight(THETA, 0, nc.vector)
            regroup_weight(THETA, 1, nc.scalar)
            quantise_x(0)
            transpose_x(1)
            project(PHI, 0)
            quantise_weight(THETA, 0)
            regroup_x(1, nc.scalar)
            for t in range(PACK):
                add_bias(PHI, 0, t)
            quantise_weight(THETA, 1)
            project_words(THETA, 0)
            quantise_x(1)
            add_bias_words(THETA, 0, 0)
            add_bias_words(THETA, 0, 1)
            regroup(PHI, 0)
            transpose_x(2)
            project(PHI, 1)
            project_words(THETA, 1)
            regroup_x(2, nc.scalar)
            for t in range(PACK):
                add_bias(PHI, 1, t)
            quantise_x(2)
            quantise(0)
            transpose_x(3)
            regroup_x(3, nc.scalar)
            project(PHI, 2)
            project_words(THETA, 2)
            for t in range(PACK):
                add_bias(PHI, 2, t)
            product(PHI, THETA, 0, 0)
            add_bias_words(THETA, 1, 0)
            add_bias_words(THETA, 1, 1)
            regroup(PHI, 1)
            quantise_x(3)
            quantise(1)
            rectify_diagonal(0)
            project(PHI, 3)
            for t in range(2):
                add_bias(PHI, 3, t)
            add_bias_words(THETA, 2, 0)
            add_bias_words(THETA, 2, 1)
            product(PHI, THETA, 1, 0)
            product(PHI, THETA, 1, 1)
            product(THETA, PHI, 1, 0)
            rectify(PHI, 1, 0)
            for t in range(2, PACK):
                add_bias(PHI, 3, t)
            rectify_diagonal(1)
            project(THETA, 3)
            transpose_blocks("term", 0, 0)
            regroup(PHI, 2)
            for t in range(PACK):
                add_bias(THETA, 3, t)
            add_up(THETA, 1, 0)
            quantise(2)
            add_diagonal(0)
            transpose_blocks("sum", 1, 0)
            transpose_blocks("term", 1, 1)
            product(PHI, THETA, 2, 0)
            product(THETA, PHI, 2, 0)
            rectify(PHI, 2, 0)
            scale(1, 0, nc.vector)
            add_diagonal(1)
            mirror(1, 0, nc.scalar)
            product(PHI, THETA, 2, 1)
            rectify(PHI, 2, 1)
            product(THETA, PHI, 2, 1)
            product(PHI, THETA, 2, 2)
            rectify_diagonal(2)
            regroup(PHI, 3)
            add_up(THETA, 2, 0)
            quantise(3, PHI, PHI)
            scale(2, 0, nc.scalar)
            transpose_blocks("sum", 2, 0)
            mirror(2, 0, nc.scalar)
            product(PHI, THETA, 3, 0)
            rectify(PHI, 3, 0)
            add_up(THETA, 2, 1)
            regroup(THETA, 3)
            scale(2, 1, nc.vector)
            transpose_blocks("sum", 2, 1)
            transpose_blocks("term", 2, 2)
            mirror(2, 1, nc.scalar)
            quantise(3, THETA, THETA)
            for n in range(1, 3):
                product(PHI, THETA, 3, n)
                rectify(PHI, 3, n)
            add_diagonal(2)
            for n in range(3):
                product(THETA, PHI, 3, n)
            product(PHI, THETA, 3, 3)
            rectify_diagonal(3)
            add_up(THETA, 3, 0)
            add_up(THETA, 3, 1)
            scale(3, 0, nc.vector)
            transpose_blocks("sum", 3, 0)
            mirror(3, 0, nc.scalar)
            add_up(THETA, 3, 2)
            scale(3, 1, nc.vector)
            transpose_blocks("sum", 3, 1)
            mirror(3, 1, nc.scalar)
            transpose_blocks("term", 3, 3)
            scale(3, 2, nc.vector)
            transpose_blocks("sum", 3, 2)
            mirror(3, 2, nc.scalar)
            add_diagonal(3)
